import numpy as np
import ml_dtypes


def mxq(x, axis, fmt="e4m3"):
    dtype, down = {"e4m3": (ml_dtypes.float8_e4m3fn, 7), "e5m2": (ml_dtypes.float8_e5m2, 14)}[fmt]
    v = np.moveaxis(np.asarray(x, np.float32).astype(ml_dtypes.bfloat16).astype(np.float64), axis, -1)
    blocks = v.reshape(v.shape[:-1] + (-1, 32))
    amax = np.abs(blocks).max(-1, keepdims=True)
    byte = np.maximum(np.where(amax > 0, np.frexp(amax)[1] - 1 + 127, 0) - down, 1)
    scale = np.exp2(byte - 127.0)
    codes = (blocks / scale).astype(np.float32).astype(dtype).astype(np.float64)
    return np.moveaxis((codes * scale).reshape(v.shape), -1, axis)


WIDE = False


def mx_kscale(k):
    if not WIDE:
        return np.ones(k)
    levels = np.array([20, -20, 10, -10, 0])
    a = np.random.permutation(np.resize(levels, k // 512 * 4)).reshape(k // 512, 4)
    idx = np.arange(k)
    return np.exp2(a[idx // 512, idx % 128 // 32])


BF16 = ml_dtypes.bfloat16


def bf(x):
    return np.asarray(x, np.float32).astype(BF16)


def f64(x):
    return np.asarray(x).astype(np.float64)


B, I, O, G = 512, 128, 1024, 3
K = I * G


def bspline_basis(d):
    inner = 1.0 - 6.0 * d * d + 6.0 * d * d * d
    outer = 2.0 * (1.0 - d) ** 3
    return np.where(d < 0.5, inner, np.where(d < 1.0, outer, np.zeros_like(d)))


def bspline_slope(d):
    inner = -12.0 * d + 18.0 * d * d
    outer = -6.0 * (1.0 - d) ** 2
    return np.where(d < 0.5, inner, np.where(d < 1.0, outer, np.zeros_like(d)))


def setup_inputs():
    g = np.linspace(-1.0, 1.0, G)
    s = mx_kscale(O)
    x_norm = np.tanh(np.random.standard_normal((B, I)))
    spline_weight = np.random.standard_normal((O, I, G)) / np.sqrt(I) / s[:, None, None]
    base_activation = np.random.standard_normal((O, I)) * 4.0 / np.sqrt(I) / s[:, None]
    grid_points = g + 0.1 * (g[1] - g[0]) * np.random.standard_normal(G)
    grad_out = np.random.standard_normal((B, O)) * np.exp2(np.random.randint(-12, 1, (B, 1))) * 4.0 * s
    return {"x_norm": bf(x_norm),
            "spline_weight": bf(spline_weight),
            "base_activation": bf(base_activation),
            "grid_points": bf(grid_points),
            "grad_out": bf(grad_out)}


def reference(x_norm, spline_weight, base_activation, grid_points, grad_out):
    t = f64(x_norm)
    diff = t[:, :, None] - f64(grid_points)
    slope = bspline_slope(np.abs(diff)) * np.sign(diff)
    gq = mxq(f64(grad_out), 1, "e5m2")
    h = gq @ mxq(f64(spline_weight).reshape(O, K), 0, "e4m3")
    base = gq @ mxq(f64(base_activation), 0, "e4m3")
    return (h.reshape(B, I, G) * slope).sum(axis=2) + 0.1 * base

@@ -1,0 +1,216 @@
+import concourse.mybir as mybir
+from concourse.masks import make_identity
+
+F32 = mybir.dt.float32
+BF16 = mybir.dt.bfloat16
+U32 = mybir.dt.uint32
+U8 = mybir.dt.uint8
+E4M3_X4 = mybir.dt.float8_e4m3fn_x4
+E5M2_X4 = mybir.dt.float8_e5m2_x4
+ALU = mybir.AluOpType
+ACT = mybir.ActivationFunctionType
+
+P = 128
+B, I, O, G = 512, 128, 1024, 3
+PACK = 4
+K_PASS = P * PACK
+PASSES = O // K_PASS
+HALVES = 2
+PAIR = 2
+ROW_TILES = B // P
+SPLINE_COLS = I * G
+W_COLS = SPLINE_COLS + I
+
+FLOPS = 2 * B * O * W_COLS
+
+
+def tile_advancedkanlayer_pa_s_kernel(
+    tc, x_norm, spline_weight, base_activation, grid_points, grad_out, out
+):
+    nc = tc.nc
+
+    spline_rows = spline_weight.rearrange(
+        "(c u p e) i g -> p c u (e i g)", c=PASSES, u=HALVES, e=PAIR
+    )
+    base_rows = base_activation.rearrange(
+        "(c u p e) i -> p c u (e i)", c=PASSES, u=HALVES, e=PAIR
+    )
+    x_rows = x_norm.rearrange("(p t) i -> p t i", t=ROW_TILES)
+    grad_rows = grad_out.rearrange("(p t) o -> p t o", t=ROW_TILES)
+    out_rows = out.rearrange("(p t) i -> p t i", t=ROW_TILES)
+
+    with tc.tile_pool(name="keep", bufs=1) as keep, tc.tile_pool(
+        name="work", bufs=ROW_TILES
+    ) as work, tc.psum_pool(name="flipped", bufs=ROW_TILES) as flipped, tc.psum_pool(
+        name="sums", bufs=ROW_TILES
+    ) as sums:
+        x_bf = keep.tile([P, ROW_TILES, I], BF16)
+        nc.sync.dma_start(out=x_bf[:], in_=x_rows)
+        grid_bf = keep.tile([P, G], BF16)
+        nc.scalar.dma_start(out=grid_bf[:], in_=grid_points.partition_broadcast(P))
+
+        spline_raw = keep.tile([P, PASSES, PACK, SPLINE_COLS], BF16)
+        base_raw = keep.tile([P, PASSES, PACK, I], BF16)
+        for c in range(PASSES):
+            nc.sync.dma_start(
+                out=spline_raw[:, c].rearrange("p (u e) w -> p u (e w)", e=PAIR),
+                in_=spline_rows[:, c],
+            )
+            nc.sync.dma_start(
+                out=base_raw[:, c].rearrange("p (u e) w -> p u (e w)", e=PAIR),
+                in_=base_rows[:, c],
+            )
+        grad_raw = keep.tile([P, ROW_TILES, O], BF16)
+        for t in range(ROW_TILES):
+            nc.sync.dma_start(out=grad_raw[:, t, :], in_=grad_rows[:, t, :])
+
+        identity = keep.tile([P, P], F32)
+        make_identity(nc, identity[:])
+
+        upper = keep.tile([P, G], F32)
+        lower = keep.tile([P, G], F32)
+        minus_18_grid = keep.tile([P, G], F32)
+        grid_f32 = keep.tile([P, G], F32)
+        nc.vector.tensor_scalar(
+            out=upper[:], in0=grid_bf[:], scalar1=2.0, scalar2=1.0, op0=ALU.mult, op1=ALU.add
+        )
+        nc.vector.tensor_scalar(
+            out=lower[:], in0=grid_bf[:], scalar1=2.0, scalar2=-1.0, op0=ALU.mult, op1=ALU.add
+        )
+        nc.vector.tensor_scalar(
+            out=minus_18_grid[:], in0=grid_bf[:], scalar1=-18.0, scalar2=None, op0=ALU.mult
+        )
+        nc.vector.tensor_copy(out=grid_f32[:], in_=grid_bf[:])
+
+        x_flat = x_bf[:].rearrange("p t i -> p (t i)")
+        twice_x = keep.tile([P, B], BF16)
+        nc.vector.tensor_scalar(
+            out=twice_x[:], in0=x_flat, scalar1=2.0, scalar2=None, op0=ALU.mult
+        )
+
+        clamped = keep.tile([P, G, B], F32)
+        plus = keep.tile([P, G, B], F32)
+        minus = keep.tile([P, G, B], F32)
+        six_abs = keep.tile([P, G, B], F32)
+        six_relu = keep.tile([P, G, B], F32)
+        slope = keep.tile([P, G, B], F32)
+        for g in range(G):
+            nc.gpsimd.tensor_scalar(
+                out=clamped[:, g, :],
+                in0=twice_x[:],
+                scalar1=upper[:, g : g + 1],
+                scalar2=lower[:, g : g + 1],
+                op0=ALU.min,
+                op1=ALU.max,
+            )
+        for g in range(G):
+            nc.vector.tensor_tensor(
+                out=plus[:, g, :], in0=clamped[:, g, :], in1=x_flat, op=ALU.add
+            )
+            nc.gpsimd.tensor_tensor(
+                out=minus[:, g, :], in0=x_flat, in1=clamped[:, g, :], op=ALU.subtract
+            )
+            nc.scalar.activation(
+                out=six_abs[:, g, :],
+                in_=plus[:, g, :],
+                func=ACT.Abs,
+                bias=minus_18_grid[:, g : g + 1],
+                scale=6.0,
+            )
+            nc.scalar.activation(
+                out=six_relu[:, g, :], in_=six_abs[:, g, :], func=ACT.Relu, bias=12.0, scale=-1.0
+            )
+
+        w_grouped = keep.tile([P, PASSES, W_COLS, PACK], BF16, align_bytes=64)
+        w_codes = keep.tile([P, PASSES, W_COLS], U32, align_bytes=64)
+        w_scales = keep.tile([P, PASSES, W_COLS], U8, align_bytes=64)
+        for c in range(PASSES):
+            nc.vector.tensor_copy(
+                out=w_grouped[:, c, 0:SPLINE_COLS, :].rearrange("p (w r) j -> p w j r", r=4),
+                in_=spline_raw[:, c].rearrange("p j (w r) -> p w j r", r=4),
+            )
+            nc.scalar.copy(
+                out=w_grouped[:, c, SPLINE_COLS:W_COLS, :].rearrange("p (w r) j -> p w j r", r=4),
+                in_=base_raw[:, c].rearrange("p j (w r) -> p w j r", r=4),
+            )
+        for c in range(PASSES):
+            nc.vector.quantize_mx(
+                out=w_codes[:, c, :].bitcast(E4M3_X4),
+                scales=w_scales[:, c, :],
+                in_=w_grouped[:, c].rearrange("p w j -> p (w j)"),
+            )
+
+        for g in range(G):
+            nc.vector.scalar_tensor_tensor(
+                out=slope[:, g, :],
+                in0=minus[:, g, :],
+                scalar=grid_f32[:, g : g + 1],
+                in1=six_relu[:, g, :],
+                op0=ALU.add,
+                op1=ALU.mult,
+            )
+
+        grad_grouped = keep.tile([P, ROW_TILES, PASSES * P * PACK], BF16, align_bytes=64)
+        grad_codes = keep.tile([P, ROW_TILES, PASSES * P], U32, align_bytes=64)
+        grad_scales = keep.tile([P, ROW_TILES, PASSES * P], U8, align_bytes=64)
+        for t in range(ROW_TILES):
+            grad_words = grad_raw[:, t, :].bitcast(F32)
+            words_t = flipped.tile([P, PASSES, HALVES, P], F32)
+            for c in range(PASSES):
+                for u in range(HALVES):
+                    first = (c * HALVES + u) * P
+                    nc.tensor.transpose(
+                        out=words_t[:, c, u, :],
+                        in_=grad_words[:, first : first + P],
+                        identity=identity[:],
+                    )
+            nc.scalar.copy(
+                out=grad_grouped[:, t, :]
+                .bitcast(F32)
+                .rearrange("p (c b u) -> p c b u", c=PASSES, u=HALVES),
+                in_=words_t[:].rearrange("p c u b -> p c b u"),
+            )
+            nc.vector.quantize_mx(
+                out=grad_codes[:, t, :].bitcast(E5M2_X4),
+                scales=grad_scales[:, t, :],
+                in_=grad_grouped[:, t, :],
+            )
+
+        out_sb = keep.tile([P, ROW_TILES, I], F32)
+        for t in range(ROW_TILES):
+            acc = sums.tile([P, W_COLS], F32)
+            for c in range(PASSES):
+                rows = slice(c * P, (c + 1) * P)
+                nc.tensor.matmul_mx(
+                    out=acc[:],
+                    lhsT=grad_codes[:, t, rows].bitcast(E5M2_X4),
+                    lhsT_scale=grad_scales[:, t, rows],
+                    rhs=w_codes[:, c, :].bitcast(E4M3_X4),
+                    rhs_scale=w_scales[:, c, :],
+                    start=(c == 0),
+                    stop=(c == PASSES - 1),
+                )
+            weighted = work.tile([P, G, I], F32)
+            nc.vector.tensor_tensor(
+                out=weighted[:],
+                in0=acc[:, 0:SPLINE_COLS].rearrange("p (i g) -> p g i", g=G),
+                in1=slope[:, :, t * I : (t + 1) * I],
+                op=ALU.mult,
+            )
+            first_two = work.tile([P, I], F32)
+            nc.vector.tensor_tensor(
+                out=first_two[:], in0=weighted[:, 0, :], in1=weighted[:, 1, :], op=ALU.add
+            )
+            third_and_base = work.tile([P, I], F32)
+            nc.vector.scalar_tensor_tensor(
+                out=third_and_base[:],
+                in0=acc[:, SPLINE_COLS:W_COLS],
+                scalar=0.1,
+                in1=weighted[:, 2, :],
+                op0=ALU.mult,
+                op1=ALU.add,
+            )
+            nc.vector.tensor_tensor(
+                out=out_sb[:, t, :], in0=first_two[:], in1=third_and_base[:], op=ALU.add
+            )
+            nc.sync.dma_start(out=out_rows[:, t, :], in_=out_sb[:, t, :])

@@ -67,58 +67,55 @@ def tile_advancedkanlayer_pa_s_kernel(
         identity = keep.tile([P, P], F32)
         make_identity(nc, identity[:])
 
-        upper = keep.tile([P, G], F32)
-        lower = keep.tile([P, G], F32)
-        minus_18_grid = keep.tile([P, G], F32)
-        grid_f32 = keep.tile([P, G], F32)
+        grid_minus_half = keep.tile([P, G], F32)
         nc.vector.tensor_scalar(
-            out=upper[:], in0=grid_bf[:], scalar1=2.0, scalar2=1.0, op0=ALU.mult, op1=ALU.add
-        )
-        nc.vector.tensor_scalar(
-            out=lower[:], in0=grid_bf[:], scalar1=2.0, scalar2=-1.0, op0=ALU.mult, op1=ALU.add
-        )
-        nc.vector.tensor_scalar(
-            out=minus_18_grid[:], in0=grid_bf[:], scalar1=-18.0, scalar2=None, op0=ALU.mult
-        )
-        nc.vector.tensor_copy(out=grid_f32[:], in_=grid_bf[:])
-
-        x_flat = x_bf[:].rearrange("p t i -> p (t i)")
-        twice_x = keep.tile([P, B], BF16)
-        nc.vector.tensor_scalar(
-            out=twice_x[:], in0=x_flat, scalar1=2.0, scalar2=None, op0=ALU.mult
+            out=grid_minus_half[:], in0=grid_bf[:], scalar1=-0.5, scalar2=None, op0=ALU.add
         )
 
-        clamped = keep.tile([P, G, B], F32)
-        plus = keep.tile([P, G, B], F32)
-        minus = keep.tile([P, G, B], F32)
-        six_abs = keep.tile([P, G, B], F32)
-        six_relu = keep.tile([P, G, B], F32)
-        slope = keep.tile([P, G, B], F32)
+        dist = keep.tile([P, ROW_TILES, G, I], F32)
+        minus_far = keep.tile([P, ROW_TILES, G, I], F32)
+        minus_near = keep.tile([P, ROW_TILES, G, I], F32)
+        six_q = keep.tile([P, ROW_TILES, G, I], F32)
+        fold_once = keep.tile([P, ROW_TILES, G, I], F32)
         for g in range(G):
-            nc.gpsimd.tensor_scalar(
-                out=clamped[:, g, :],
-                in0=twice_x[:],
-                scalar1=upper[:, g : g + 1],
-                scalar2=lower[:, g : g + 1],
-                op0=ALU.min,
+            nc.scalar.activation(
+                out=dist[:, :, g, :],
+                in_=x_bf[:],
+                func=ACT.Abs,
+                bias=grid_bf[:, g : g + 1],
+                scale=-1.0,
+            )
+            nc.vector.tensor_scalar(
+                out=minus_far[:, :, g, :],
+                in0=dist[:, :, g, :],
+                scalar1=-6.0,
+                scalar2=-6.0,
+                op0=ALU.mult,
                 op1=ALU.max,
             )
+            nc.vector.tensor_scalar(
+                out=minus_near[:, :, g, :],
+                in0=dist[:, :, g, :],
+                scalar1=-12.0,
+                scalar2=-6.0,
+                op0=ALU.mult,
+                op1=ALU.max,
+            )
+            nc.vector.scalar_tensor_tensor(
+                out=six_q[:, :, g, :],
+                in0=minus_far[:, :, g, :],
+                scalar=12.0,
+                in1=minus_near[:, :, g, :],
+                op0=ALU.add,
+                op1=ALU.add,
+            )
         for g in range(G):
-            nc.vector.tensor_tensor(
-                out=plus[:, g, :], in0=clamped[:, g, :], in1=x_flat, op=ALU.add
-            )
-            nc.gpsimd.tensor_tensor(
-                out=minus[:, g, :], in0=x_flat, in1=clamped[:, g, :], op=ALU.subtract
-            )
             nc.scalar.activation(
-                out=six_abs[:, g, :],
-                in_=plus[:, g, :],
+                out=fold_once[:, :, g, :],
+                in_=x_bf[:],
                 func=ACT.Abs,
-                bias=minus_18_grid[:, g : g + 1],
-                scale=6.0,
-            )
-            nc.scalar.activation(
-                out=six_relu[:, g, :], in_=six_abs[:, g, :], func=ACT.Relu, bias=12.0, scale=-1.0
+                bias=grid_minus_half[:, g : g + 1],
+                scale=-1.0,
             )
 
         w_grouped = keep.tile([P, PASSES, W_COLS, PACK], BF16, align_bytes=64)
@@ -140,19 +137,11 @@ def tile_advancedkanlayer_pa_s_kernel(
                 in_=w_grouped[:, c].rearrange("p w j -> p (w j)"),
             )
 
-        for g in range(G):
-            nc.vector.scalar_tensor_tensor(
-                out=slope[:, g, :],
-                in0=minus[:, g, :],
-                scalar=grid_f32[:, g : g + 1],
-                in1=six_relu[:, g, :],
-                op0=ALU.add,
-                op1=ALU.mult,
-            )
-
         grad_grouped = keep.tile([P, ROW_TILES, PASSES * P * PACK], BF16, align_bytes=64)
         grad_codes = keep.tile([P, ROW_TILES, PASSES * P], U32, align_bytes=64)
         grad_scales = keep.tile([P, ROW_TILES, PASSES * P], U8, align_bytes=64)
+        fold_twice = keep.tile([P, ROW_TILES, SPLINE_COLS], F32)
+        slope = keep.tile([P, ROW_TILES, G, I], F32)
         for t in range(ROW_TILES):
             grad_words = grad_raw[:, t, :].bitcast(F32)
             words_t = flipped.tile([P, PASSES, HALVES, P], F32)
@@ -175,6 +164,21 @@ def tile_advancedkanlayer_pa_s_kernel(
                 scales=grad_scales[:, t, :],
                 in_=grad_grouped[:, t, :],
             )
+            nc.scalar.activation(
+                out=fold_twice[:, t, :],
+                in_=fold_once[:, t].rearrange("p g i -> p (g i)"),
+                func=ACT.Abs,
+                bias=-1.0,
+                scale=1.0,
+            )
+            nc.vector.scalar_tensor_tensor(
+                out=slope[:, t].rearrange("p g i -> p (g i)"),
+                in0=fold_twice[:, t, :],
+                scalar=-0.5,
+                in1=six_q[:, t].rearrange("p g i -> p (g i)"),
+                op0=ALU.add,
+                op1=ALU.mult,
+            )
 
         out_sb = keep.tile([P, ROW_TILES, I], F32)
         for t in range(ROW_TILES):
@@ -194,7 +198,7 @@ def tile_advancedkanlayer_pa_s_kernel(
             nc.vector.tensor_tensor(
                 out=weighted[:],
                 in0=acc[:, 0:SPLINE_COLS].rearrange("p (i g) -> p g i", g=G),
-                in1=slope[:, :, t * I : (t + 1) * I],
+                in1=slope[:, t],
                 op=ALU.mult,
             )
             first_two = work.tile([P, I], F32)

@@ -20,6 +20,7 @@ PAIR = 2
 ROW_TILES = B // P
 SPLINE_COLS = I * G
 W_COLS = SPLINE_COLS + I
+VECTOR_COLS = 256
 
 FLOPS = 2 * B * O * W_COLS
 
@@ -48,6 +49,11 @@ def tile_advancedkanlayer_pa_s_kernel(
         nc.sync.dma_start(out=x_bf[:], in_=x_rows)
         grid_bf = keep.tile([P, G], BF16)
         nc.scalar.dma_start(out=grid_bf[:], in_=grid_points.partition_broadcast(P))
+
+        table_in = keep.tile([P, 1], F32)
+        table_out = keep.tile([P, 1], F32)
+        nc.gpsimd.memset(table_in[:], 0.0)
+        nc.scalar.activation(out=table_out[:], in_=table_in[:], func=ACT.Abs)
 
         spline_raw = keep.tile([P, PASSES, PACK, SPLINE_COLS], BF16)
         base_raw = keep.tile([P, PASSES, PACK, I], BF16)
@@ -123,8 +129,16 @@ def tile_advancedkanlayer_pa_s_kernel(
         w_scales = keep.tile([P, PASSES, W_COLS], U8, align_bytes=64)
         for c in range(PASSES):
             nc.vector.tensor_copy(
-                out=w_grouped[:, c, 0:SPLINE_COLS, :].rearrange("p (w r) j -> p w j r", r=4),
-                in_=spline_raw[:, c].rearrange("p j (w r) -> p w j r", r=4),
+                out=w_grouped[:, c, 0:VECTOR_COLS, :].rearrange("p (w r) j -> p w j r", r=4),
+                in_=spline_raw[:, c, :, 0:VECTOR_COLS].rearrange("p j (w r) -> p w j r", r=4),
+            )
+            nc.scalar.copy(
+                out=w_grouped[:, c, VECTOR_COLS:SPLINE_COLS, :].rearrange(
+                    "p (w r) j -> p w j r", r=4
+                ),
+                in_=spline_raw[:, c, :, VECTOR_COLS:SPLINE_COLS].rearrange(
+                    "p j (w r) -> p w j r", r=4
+                ),
             )
             nc.scalar.copy(
                 out=w_grouped[:, c, SPLINE_COLS:W_COLS, :].rearrange("p (w r) j -> p w j r", r=4),

@@ -1,3 +1,5 @@
+from contextlib import ExitStack
+
 import concourse.mybir as mybir
 from concourse.masks import make_identity
 
@@ -20,7 +22,6 @@ PAIR = 2
 ROW_TILES = B // P
 SPLINE_COLS = I * G
 W_COLS = SPLINE_COLS + I
-VECTOR_COLS = 256
 
 FLOPS = 2 * B * O * W_COLS
 
@@ -40,11 +41,14 @@ def tile_advancedkanlayer_pa_s_kernel(
     grad_rows = grad_out.rearrange("(p t) o -> p t o", t=ROW_TILES)
     out_rows = out.rearrange("(p t) i -> p t i", t=ROW_TILES)
 
-    with tc.tile_pool(name="keep", bufs=1) as keep, tc.tile_pool(
-        name="work", bufs=ROW_TILES
-    ) as work, tc.psum_pool(name="flipped", bufs=ROW_TILES) as flipped, tc.psum_pool(
-        name="sums", bufs=ROW_TILES
-    ) as sums:
+    with tc.tile_pool(name="keep", bufs=1) as keep, tc.psum_pool(
+        name="flipped", bufs=ROW_TILES
+    ) as flipped, tc.psum_pool(name="sums", bufs=ROW_TILES) as sums, ExitStack() as written_order:
+        identity = keep.tile([P, P], F32)
+        make_identity(nc, identity[:])
+
+        written_order.enter_context(tc.manual_schedule())
+
         x_bf = keep.tile([P, ROW_TILES, I], BF16)
         nc.sync.dma_start(out=x_bf[:], in_=x_rows)
         grid_bf = keep.tile([P, G], BF16)
@@ -70,9 +74,6 @@ def tile_advancedkanlayer_pa_s_kernel(
         for t in range(ROW_TILES):
             nc.sync.dma_start(out=grad_raw[:, t, :], in_=grad_rows[:, t, :])
 
-        identity = keep.tile([P, P], F32)
-        make_identity(nc, identity[:])
-
         grid_minus_half = keep.tile([P, G], F32)
         nc.vector.tensor_scalar(
             out=grid_minus_half[:], in0=grid_bf[:], scalar1=-0.5, scalar2=None, op0=ALU.add
@@ -83,6 +84,35 @@ def tile_advancedkanlayer_pa_s_kernel(
         minus_near = keep.tile([P, ROW_TILES, G, I], F32)
         six_q = keep.tile([P, ROW_TILES, G, I], F32)
         fold_once = keep.tile([P, ROW_TILES, G, I], F32)
+        fold_twice = keep.tile([P, ROW_TILES, SPLINE_COLS], F32)
+        slope = keep.tile([P, ROW_TILES, G, I], F32)
+
+        w_grouped = keep.tile([P, PASSES, W_COLS, PACK], BF16, align_bytes=64)
+        w_codes = keep.tile([P, PASSES, W_COLS], U32, align_bytes=64)
+        w_scales = keep.tile([P, PASSES, W_COLS], U8, align_bytes=64)
+
+        def add_six_q_terms(g):
+            nc.vector.scalar_tensor_tensor(
+                out=six_q[:, :, g, :],
+                in0=minus_far[:, :, g, :],
+                scalar=12.0,
+                in1=minus_near[:, :, g, :],
+                op0=ALU.add,
+                op1=ALU.add,
+            )
+
+        def group_spline_rows(c):
+            nc.vector.tensor_copy(
+                out=w_grouped[:, c, 0:SPLINE_COLS, :].rearrange("p (w r) j -> p w j r", r=4),
+                in_=spline_raw[:, c].rearrange("p j (w r) -> p w j r", r=4),
+            )
+
+        def group_base_rows(c):
+            nc.scalar.copy(
+                out=w_grouped[:, c, SPLINE_COLS:W_COLS, :].rearrange("p (w r) j -> p w j r", r=4),
+                in_=base_raw[:, c].rearrange("p j (w r) -> p w j r", r=4),
+            )
+
         for g in range(G):
             nc.scalar.activation(
                 out=dist[:, :, g, :],
@@ -107,14 +137,11 @@ def tile_advancedkanlayer_pa_s_kernel(
                 op0=ALU.mult,
                 op1=ALU.max,
             )
-            nc.vector.scalar_tensor_tensor(
-                out=six_q[:, :, g, :],
-                in0=minus_far[:, :, g, :],
-                scalar=12.0,
-                in1=minus_near[:, :, g, :],
-                op0=ALU.add,
-                op1=ALU.add,
-            )
+            if g > 0:
+                add_six_q_terms(g - 1)
+        group_base_rows(0)
+        group_spline_rows(0)
+        add_six_q_terms(G - 1)
         for g in range(G):
             nc.scalar.activation(
                 out=fold_once[:, :, g, :],
@@ -123,27 +150,8 @@ def tile_advancedkanlayer_pa_s_kernel(
                 bias=grid_minus_half[:, g : g + 1],
                 scale=-1.0,
             )
-
-        w_grouped = keep.tile([P, PASSES, W_COLS, PACK], BF16, align_bytes=64)
-        w_codes = keep.tile([P, PASSES, W_COLS], U32, align_bytes=64)
-        w_scales = keep.tile([P, PASSES, W_COLS], U8, align_bytes=64)
-        for c in range(PASSES):
-            nc.vector.tensor_copy(
-                out=w_grouped[:, c, 0:VECTOR_COLS, :].rearrange("p (w r) j -> p w j r", r=4),
-                in_=spline_raw[:, c, :, 0:VECTOR_COLS].rearrange("p j (w r) -> p w j r", r=4),
-            )
-            nc.scalar.copy(
-                out=w_grouped[:, c, VECTOR_COLS:SPLINE_COLS, :].rearrange(
-                    "p (w r) j -> p w j r", r=4
-                ),
-                in_=spline_raw[:, c, :, VECTOR_COLS:SPLINE_COLS].rearrange(
-                    "p j (w r) -> p w j r", r=4
-                ),
-            )
-            nc.scalar.copy(
-                out=w_grouped[:, c, SPLINE_COLS:W_COLS, :].rearrange("p (w r) j -> p w j r", r=4),
-                in_=base_raw[:, c].rearrange("p j (w r) -> p w j r", r=4),
-            )
+        group_base_rows(1)
+        group_spline_rows(1)
         for c in range(PASSES):
             nc.vector.quantize_mx(
                 out=w_codes[:, c, :].bitcast(E4M3_X4),
@@ -154,8 +162,6 @@ def tile_advancedkanlayer_pa_s_kernel(
         grad_grouped = keep.tile([P, ROW_TILES, PASSES * P * PACK], BF16, align_bytes=64)
         grad_codes = keep.tile([P, ROW_TILES, PASSES * P], U32, align_bytes=64)
         grad_scales = keep.tile([P, ROW_TILES, PASSES * P], U8, align_bytes=64)
-        fold_twice = keep.tile([P, ROW_TILES, SPLINE_COLS], F32)
-        slope = keep.tile([P, ROW_TILES, G, I], F32)
         for t in range(ROW_TILES):
             grad_words = grad_raw[:, t, :].bitcast(F32)
             words_t = flipped.tile([P, PASSES, HALVES, P], F32)
@@ -194,13 +200,13 @@ def tile_advancedkanlayer_pa_s_kernel(
                 op1=ALU.mult,
             )
 
-        out_sb = keep.tile([P, ROW_TILES, I], F32)
+        acc = []
         for t in range(ROW_TILES):
-            acc = sums.tile([P, W_COLS], F32)
+            acc.append(sums.tile([P, W_COLS], F32, name="acc"))
             for c in range(PASSES):
                 rows = slice(c * P, (c + 1) * P)
                 nc.tensor.matmul_mx(
-                    out=acc[:],
+                    out=acc[t][:],
                     lhsT=grad_codes[:, t, rows].bitcast(E5M2_X4),
                     lhsT_scale=grad_scales[:, t, rows],
                     rhs=w_codes[:, c, :].bitcast(E4M3_X4),
@@ -208,27 +214,40 @@ def tile_advancedkanlayer_pa_s_kernel(
                     start=(c == 0),
                     stop=(c == PASSES - 1),
                 )
-            weighted = work.tile([P, G, I], F32)
-            nc.vector.tensor_tensor(
-                out=weighted[:],
-                in0=acc[:, 0:SPLINE_COLS].rearrange("p (i g) -> p g i", g=G),
-                in1=slope[:, t],
-                op=ALU.mult,
-            )
-            first_two = work.tile([P, I], F32)
-            nc.vector.tensor_tensor(
-                out=first_two[:], in0=weighted[:, 0, :], in1=weighted[:, 1, :], op=ALU.add
-            )
-            third_and_base = work.tile([P, I], F32)
-            nc.vector.scalar_tensor_tensor(
-                out=third_and_base[:],
-                in0=acc[:, SPLINE_COLS:W_COLS],
-                scalar=0.1,
-                in1=weighted[:, 2, :],
-                op0=ALU.mult,
-                op1=ALU.add,
-            )
-            nc.vector.tensor_tensor(
-                out=out_sb[:, t, :], in0=first_two[:], in1=third_and_base[:], op=ALU.add
-            )
-            nc.sync.dma_start(out=out_rows[:, t, :], in_=out_sb[:, t, :])
+
+        weighted = keep.tile([P, ROW_TILES, G, I], F32)
+        first_two = keep.tile([P, ROW_TILES, I], F32)
+        third_and_base = keep.tile([P, ROW_TILES, I], F32)
+        out_sb = keep.tile([P, ROW_TILES, I], F32)
+        for pair in range(0, ROW_TILES, 2):
+            both = (pair, pair + 1)
+            for t in both:
+                nc.vector.tensor_tensor(
+                    out=weighted[:, t],
+                    in0=acc[t][:, 0:SPLINE_COLS].rearrange("p (i g) -> p g i", g=G),
+                    in1=slope[:, t],
+                    op=ALU.mult,
+                )
+            for t in both:
+                nc.vector.tensor_tensor(
+                    out=first_two[:, t, :],
+                    in0=weighted[:, t, 0, :],
+                    in1=weighted[:, t, 1, :],
+                    op=ALU.add,
+                )
+                nc.vector.scalar_tensor_tensor(
+                    out=third_and_base[:, t, :],
+                    in0=acc[t][:, SPLINE_COLS:W_COLS],
+                    scalar=0.1,
+                    in1=weighted[:, t, 2, :],
+                    op0=ALU.mult,
+                    op1=ALU.add,
+                )
+            for t in both:
+                nc.vector.tensor_tensor(
+                    out=out_sb[:, t, :],
+                    in0=first_two[:, t, :],
+                    in1=third_and_base[:, t, :],
+                    op=ALU.add,
+                )
+                nc.sync.dma_start(out=out_rows[:, t, :], in_=out_sb[:, t, :])

from contextlib import ExitStack

import concourse.mybir as mybir
from concourse.masks import make_identity

F32 = mybir.dt.float32
BF16 = mybir.dt.bfloat16
U32 = mybir.dt.uint32
U8 = mybir.dt.uint8
E4M3_X4 = mybir.dt.float8_e4m3fn_x4
E5M2_X4 = mybir.dt.float8_e5m2_x4
ALU = mybir.AluOpType
ACT = mybir.ActivationFunctionType

P = 128
B, I, O, G = 512, 128, 1024, 3
PACK = 4
K_PASS = P * PACK
PASSES = O // K_PASS
HALVES = 2
PAIR = 2
ROW_TILES = B // P
SPLINE_COLS = I * G
W_COLS = SPLINE_COLS + I

FLOPS = 2 * B * O * W_COLS


def tile_advancedkanlayer_pa_s_kernel(
    tc, x_norm, spline_weight, base_activation, grid_points, grad_out, out
):
    nc = tc.nc

    spline_rows = spline_weight.rearrange(
        "(c u p e) i g -> p c u (e i g)", c=PASSES, u=HALVES, e=PAIR
    )
    base_rows = base_activation.rearrange(
        "(c u p e) i -> p c u (e i)", c=PASSES, u=HALVES, e=PAIR
    )
    x_rows = x_norm.rearrange("(p t) i -> p t i", t=ROW_TILES)
    grad_rows = grad_out.rearrange("(p t) o -> p t o", t=ROW_TILES)
    out_rows = out.rearrange("(p t) i -> p t i", t=ROW_TILES)

    with tc.tile_pool(name="keep", bufs=1) as keep, tc.psum_pool(
        name="flipped", bufs=ROW_TILES
    ) as flipped, tc.psum_pool(name="sums", bufs=ROW_TILES) as sums, ExitStack() as written_order:
        identity = keep.tile([P, P], F32)
        make_identity(nc, identity[:])

        written_order.enter_context(tc.manual_schedule())

        x_bf = keep.tile([P, ROW_TILES, I], BF16)
        nc.sync.dma_start(out=x_bf[:], in_=x_rows)
        grid_bf = keep.tile([P, G], BF16)
        nc.scalar.dma_start(out=grid_bf[:], in_=grid_points.partition_broadcast(P))

        table_in = keep.tile([P, 1], F32)
        table_out = keep.tile([P, 1], F32)
        nc.gpsimd.memset(table_in[:], 0.0)
        nc.scalar.activation(out=table_out[:], in_=table_in[:], func=ACT.Abs)

        spline_raw = keep.tile([P, PASSES, PACK, SPLINE_COLS], BF16)
        base_raw = keep.tile([P, PASSES, PACK, I], BF16)
        for c in range(PASSES):
            nc.sync.dma_start(
                out=spline_raw[:, c].rearrange("p (u e) w -> p u (e w)", e=PAIR),
                in_=spline_rows[:, c],
            )
            nc.sync.dma_start(
                out=base_raw[:, c].rearrange("p (u e) w -> p u (e w)", e=PAIR),
                in_=base_rows[:, c],
            )
        grad_raw = keep.tile([P, ROW_TILES, O], BF16)
        for t in range(ROW_TILES):
            nc.sync.dma_start(out=grad_raw[:, t, :], in_=grad_rows[:, t, :])

        grid_minus_half = keep.tile([P, G], F32)
        nc.vector.tensor_scalar(
            out=grid_minus_half[:], in0=grid_bf[:], scalar1=-0.5, scalar2=None, op0=ALU.add
        )

        dist = keep.tile([P, ROW_TILES, G, I], F32)
        minus_far = keep.tile([P, ROW_TILES, G, I], F32)
        minus_near = keep.tile([P, ROW_TILES, G, I], F32)
        six_q = keep.tile([P, ROW_TILES, G, I], F32)
        fold_once = keep.tile([P, ROW_TILES, G, I], F32)
        fold_twice = keep.tile([P, ROW_TILES, SPLINE_COLS], F32)
        slope = keep.tile([P, ROW_TILES, G, I], F32)

        w_grouped = keep.tile([P, PASSES, W_COLS, PACK], BF16, align_bytes=64)
        w_codes = keep.tile([P, PASSES, W_COLS], U32, align_bytes=64)
        w_scales = keep.tile([P, PASSES, W_COLS], U8, align_bytes=64)

        def add_six_q_terms(g):
            nc.vector.scalar_tensor_tensor(
                out=six_q[:, :, g, :],
                in0=minus_far[:, :, g, :],
                scalar=12.0,
                in1=minus_near[:, :, g, :],
                op0=ALU.add,
                op1=ALU.add,
            )

        def group_spline_rows(c):
            nc.vector.tensor_copy(
                out=w_grouped[:, c, 0:SPLINE_COLS, :].rearrange("p (w r) j -> p w j r", r=4),
                in_=spline_raw[:, c].rearrange("p j (w r) -> p w j r", r=4),
            )

        def group_base_rows(c):
            nc.scalar.copy(
                out=w_grouped[:, c, SPLINE_COLS:W_COLS, :].rearrange("p (w r) j -> p w j r", r=4),
                in_=base_raw[:, c].rearrange("p j (w r) -> p w j r", r=4),
            )

        for g in range(G):
            nc.scalar.activation(
                out=dist[:, :, g, :],
                in_=x_bf[:],
                func=ACT.Abs,
                bias=grid_bf[:, g : g + 1],
                scale=-1.0,
            )
            nc.vector.tensor_scalar(
                out=minus_far[:, :, g, :],
                in0=dist[:, :, g, :],
                scalar1=-6.0,
                scalar2=-6.0,
                op0=ALU.mult,
                op1=ALU.max,
            )
            nc.vector.tensor_scalar(
                out=minus_near[:, :, g, :],
                in0=dist[:, :, g, :],
                scalar1=-12.0,
                scalar2=-6.0,
                op0=ALU.mult,
                op1=ALU.max,
            )
            if g > 0:
                add_six_q_terms(g - 1)
        group_base_rows(0)
        group_spline_rows(0)
        add_six_q_terms(G - 1)
        for g in range(G):
            nc.scalar.activation(
                out=fold_once[:, :, g, :],
                in_=x_bf[:],
                func=ACT.Abs,
                bias=grid_minus_half[:, g : g + 1],
                scale=-1.0,
            )
        group_base_rows(1)
        group_spline_rows(1)
        for c in range(PASSES):
            nc.vector.quantize_mx(
                out=w_codes[:, c, :].bitcast(E4M3_X4),
                scales=w_scales[:, c, :],
                in_=w_grouped[:, c].rearrange("p w j -> p (w j)"),
            )

        grad_grouped = keep.tile([P, ROW_TILES, PASSES * P * PACK], BF16, align_bytes=64)
        grad_codes = keep.tile([P, ROW_TILES, PASSES * P], U32, align_bytes=64)
        grad_scales = keep.tile([P, ROW_TILES, PASSES * P], U8, align_bytes=64)
        for t in range(ROW_TILES):
            grad_words = grad_raw[:, t, :].bitcast(F32)
            words_t = flipped.tile([P, PASSES, HALVES, P], F32)
            for c in range(PASSES):
                for u in range(HALVES):
                    first = (c * HALVES + u) * P
                    nc.tensor.transpose(
                        out=words_t[:, c, u, :],
                        in_=grad_words[:, first : first + P],
                        identity=identity[:],
                    )
            nc.scalar.copy(
                out=grad_grouped[:, t, :]
                .bitcast(F32)
                .rearrange("p (c b u) -> p c b u", c=PASSES, u=HALVES),
                in_=words_t[:].rearrange("p c u b -> p c b u"),
            )
            nc.vector.quantize_mx(
                out=grad_codes[:, t, :].bitcast(E5M2_X4),
                scales=grad_scales[:, t, :],
                in_=grad_grouped[:, t, :],
            )
            nc.scalar.activation(
                out=fold_twice[:, t, :],
                in_=fold_once[:, t].rearrange("p g i -> p (g i)"),
                func=ACT.Abs,
                bias=-1.0,
                scale=1.0,
            )
            nc.vector.scalar_tensor_tensor(
                out=slope[:, t].rearrange("p g i -> p (g i)"),
                in0=fold_twice[:, t, :],
                scalar=-0.5,
                in1=six_q[:, t].rearrange("p g i -> p (g i)"),
                op0=ALU.add,
                op1=ALU.mult,
            )

        acc = []
        for t in range(ROW_TILES):
            acc.append(sums.tile([P, W_COLS], F32, name="acc"))
            for c in range(PASSES):
                rows = slice(c * P, (c + 1) * P)
                nc.tensor.matmul_mx(
                    out=acc[t][:],
                    lhsT=grad_codes[:, t, rows].bitcast(E5M2_X4),
                    lhsT_scale=grad_scales[:, t, rows],
                    rhs=w_codes[:, c, :].bitcast(E4M3_X4),
                    rhs_scale=w_scales[:, c, :],
                    start=(c == 0),
                    stop=(c == PASSES - 1),
                )

        weighted = keep.tile([P, ROW_TILES, G, I], F32)
        first_two = keep.tile([P, ROW_TILES, I], F32)
        third_and_base = keep.tile([P, ROW_TILES, I], F32)
        out_sb = keep.tile([P, ROW_TILES, I], F32)
        for pair in range(0, ROW_TILES, 2):
            both = (pair, pair + 1)
            for t in both:
                nc.vector.tensor_tensor(
                    out=weighted[:, t],
                    in0=acc[t][:, 0:SPLINE_COLS].rearrange("p (i g) -> p g i", g=G),
                    in1=slope[:, t],
                    op=ALU.mult,
                )
            for t in both:
                nc.vector.tensor_tensor(
                    out=first_two[:, t, :],
                    in0=weighted[:, t, 0, :],
                    in1=weighted[:, t, 1, :],
                    op=ALU.add,
                )
                nc.vector.scalar_tensor_tensor(
                    out=third_and_base[:, t, :],
                    in0=acc[t][:, SPLINE_COLS:W_COLS],
                    scalar=0.1,
                    in1=weighted[:, t, 2, :],
                    op0=ALU.mult,
                    op1=ALU.add,
                )
            for t in both:
                nc.vector.tensor_tensor(
                    out=out_sb[:, t, :],
                    in0=first_two[:, t, :],
                    in1=third_and_base[:, t, :],
                    op=ALU.add,
                )
                nc.sync.dma_start(out=out_rows[:, t, :], in_=out_sb[:, t, :])
